import numpy as np
import ml_dtypes


def mxq(x, axis, fmt="e4m3"):
    dtype, down = {"e4m3": (ml_dtypes.float8_e4m3fn, 7), "e5m2": (ml_dtypes.float8_e5m2, 14)}[fmt]
    v = np.moveaxis(np.asarray(x, np.float32).astype(ml_dtypes.bfloat16).astype(np.float64), axis, -1)
    blocks = v.reshape(v.shape[:-1] + (-1, 32))
    amax = np.abs(blocks).max(-1, keepdims=True)
    byte = np.maximum(np.where(amax > 0, np.frexp(amax)[1] - 1 + 127, 0) - down, 1)
    scale = np.exp2(byte - 127.0)
    codes = (blocks / scale).astype(np.float32).astype(dtype).astype(np.float64)
    return np.moveaxis((codes * scale).reshape(v.shape), -1, axis)


WIDE = False


def mx_kscale(k):
    if not WIDE:
        return np.ones(k)
    levels = np.array([10, -10, 5, -5, 0])
    if k % 512:
        return np.exp2(np.random.permutation(np.resize(levels, k // 32))).repeat(32)
    a = np.empty((k // 512, 16))
    for p in range(k // 512):
        a[p, :8] = np.random.permutation(np.resize(levels, 8))
        for g in range(8):
            far = levels[np.abs(levels - a[p, g]) >= 10]
            a[p, g + 8] = far[np.random.randint(len(far))]
    return np.exp2(a.ravel()).repeat(32)


BF16 = ml_dtypes.bfloat16


def bf(x):
    return np.asarray(x, np.float32).astype(BF16)


def f64(x):
    return np.asarray(x).astype(np.float64)


B, T, C, H, D, R = 4, 1024, 1024, 8, 128, 512
EPS = 1e-6
THETA = 10000.0


def rmsnorm(v, w):
    var = np.mean(v * v, axis=-1, keepdims=True)
    return v * (1.0 / np.sqrt(var + EPS)) * w


def rope(v, cos, sin):
    re, im = v[..., 0::2], v[..., 1::2]
    c, s = cos[None, :, None, :], sin[None, :, None, :]
    return np.stack([re * c - im * s, re * s + im * c], axis=-1).reshape(v.shape)


def setup_inputs():
    s = mx_kscale(C)
    ang = np.outer(np.arange(T), 1.0 / THETA ** (np.arange(0, D, 2) / D))
    return {"x": bf(np.random.standard_normal((B, T, C)) * s),
            "wq": bf(np.random.standard_normal((H * D, C)) / np.sqrt(C) / s[None, :]),
            "q_norm_w": bf(1.0 + 0.1 * np.random.standard_normal(D)),
            "freqs_cos": bf(np.cos(ang)), "freqs_sin": bf(np.sin(ang))}


def reference(x, wq, q_norm_w, freqs_cos, freqs_sin):
    xq = (mxq(f64(x), 2, "e4m3") @ mxq(f64(wq), 1, "e4m3").T).reshape(B, T, H, D)
    return rope(rmsnorm(xq, f64(q_norm_w)), f64(freqs_cos), f64(freqs_sin))

@@ -1,0 +1,265 @@
+from contextlib import ExitStack
+
+import concourse.mybir as mybir
+from concourse.masks import make_identity
+
+F32 = mybir.dt.float32
+BF16 = mybir.dt.bfloat16
+U32 = mybir.dt.uint32
+U8 = mybir.dt.uint8
+FP8X4 = mybir.dt.float8_e4m3fn_x4
+ACT = mybir.ActivationFunctionType
+ALU = mybir.AluOpType
+
+P = 128
+TOKENS = 4 * 1024
+SEQUENCE = 1024
+K = 1024
+HEADS = 8
+HEAD_DIM = 128
+PAIRS = HEAD_DIM // 2
+FEATURES = HEADS * HEAD_DIM
+EPS = 1e-6
+
+PACK = 4
+PASSES = K // (P * PACK)
+HALVES = 2
+WORD_BLOCKS = PASSES * HALVES
+BANK = 512
+BANKS = FEATURES // BANK
+HEADS_PER_BANK = BANK // HEAD_DIM
+GROUP = 4
+TILES = TOKENS // P
+TABLES = SEQUENCE // P
+
+FLOPS = 2 * TOKENS * K * FEATURES
+
+
+def tile_mla_pb_t_kernel(tc, x, wq, q_norm_w, freqs_cos, freqs_sin, out):
+    nc = tc.nc
+    x_rows = x.flatten_outer_dims()
+    out_rows = out.rearrange("b t h d -> (b t) (h d)")
+
+    with ExitStack() as stack:
+        keep = stack.enter_context(tc.tile_pool(name="keep", bufs=1))
+        stage = stack.enter_context(tc.tile_pool(name="stage", bufs=2))
+        work = stack.enter_context(tc.tile_pool(name="work", bufs=3))
+        results = stack.enter_context(tc.tile_pool(name="results", bufs=4))
+        psum_turned = stack.enter_context(tc.psum_pool(name="psum_turned", bufs=2))
+        psum_q = stack.enter_context(tc.psum_pool(name="psum_q", bufs=3 * BANKS))
+        stack.enter_context(tc.manual_schedule())
+
+        gain_row = keep.tile([P, HEAD_DIM], BF16)
+        nc.vector.memset(gain_row[:], 0.0)
+        nc.sync.dma_start(out=gain_row[0:1, :], in_=q_norm_w.unsqueeze(0))
+        cos = keep.tile([P, TABLES // GROUP, GROUP * PAIRS], BF16)
+        sin = keep.tile([P, TABLES // GROUP, GROUP * PAIRS], BF16)
+        for table, freqs in ((cos, freqs_cos), (sin, freqs_sin)):
+            nc.scalar.dma_start(out=table[:], in_=freqs.rearrange("(s p i) j -> p s (i j)", p=P, i=GROUP))
+
+        wq_sb = keep.tile([P, HEADS, K], BF16)
+        wq_by_head = wq.rearrange("(h p) k -> p h k", p=P)
+        for h in range(HEADS):
+            nc.sync.dma_start(out=wq_sb[:, h, :], in_=wq_by_head[:, h, :])
+        x_sb = keep.tile([P, TILES, K], BF16)
+        for first in range(0, TILES, GROUP):
+            x_group = x_rows[first * P : (first + GROUP) * P, :].rearrange("(p i) k -> p i k", i=GROUP)
+            if first == 0:
+                for i in range(GROUP):
+                    nc.sync.dma_start(out=x_sb[:, i, :], in_=x_group[:, i, :])
+            else:
+                nc.sync.dma_start(out=x_sb[:, first : first + GROUP, :], in_=x_group)
+
+        eps = keep.tile([P, 1], F32)
+        nc.vector.memset(eps[:], EPS)
+        first_use = keep.tile([P, 1], F32)
+        nc.scalar.activation(out=first_use[:], in_=eps[:], func=ACT.Abs_reciprocal_sqrt)
+
+        identity = keep.tile([P, P], F32)
+        make_identity(nc, identity[:])
+        evens_first = keep.tile([P, P], F32)
+        nc.vector.tensor_copy(
+            out=evens_first[:].rearrange("p (a j) -> p a j", a=2),
+            in_=identity[:].rearrange("p (j a) -> p a j", a=2),
+        )
+
+        ones = keep.tile([P, P], BF16)
+        nc.vector.memset(ones[:], 1.0)
+        gain_bank = psum_turned.tile([P, WORD_BLOCKS, P], F32, tag="turned")
+        nc.tensor.matmul(out=gain_bank[:, 0, :], lhsT=ones[:], rhs=gain_row[:], start=True, stop=True)
+        gain = keep.tile([P, HEAD_DIM], F32)
+        nc.vector.tensor_copy(out=gain[:], in_=gain_bank[:, 0, :])
+
+        neg_sin = keep.tile([P, TABLES // GROUP, GROUP * PAIRS], BF16)
+        nc.gpsimd.tensor_scalar(out=neg_sin[:], in0=sin[:], scalar1=-1.0, scalar2=0.0, op0=ALU.mult, op1=ALU.add)
+        rot = keep.tile([P, TABLES, 2 * HEAD_DIM], F32)
+        rot_parts = rot[:].rearrange("p m (a j e) -> p e a m j", a=2, e=2)
+        gain_parts = gain[:].rearrange("p (j a) -> p a j", a=2)
+        for e, a, trig in ((0, 0, cos), (0, 1, neg_sin), (1, 0, sin), (1, 1, cos)):
+            nc.gpsimd.tensor_tensor(
+                out=rot_parts[:, e, a],
+                in0=trig[:].rearrange("p s (i j) -> p (s i) j", i=GROUP),
+                in1=gain_parts[:, a].unsqueeze(1).to_broadcast([P, TABLES, PAIRS]),
+                op=ALU.mult,
+            )
+
+        def turn(rows, selector):
+            turned = psum_turned.tile([P, WORD_BLOCKS, P], F32)
+            words = rows.bitcast(F32)
+            for g in range(PASSES):
+                first, last = g * HALVES * P, (g + 1) * HALVES * P
+                for u in range(HALVES):
+                    nc.tensor.transpose(turned[:, g * HALVES + u, :], words[:, first + u : last : HALVES], selector[:])
+            return turned
+
+        def by_packed_word(turned):
+            return turned[:].rearrange("p (g u) r -> p g r u", u=HALVES)
+
+        w_codes = keep.tile([P, PASSES, FEATURES], U32, align_bytes=64)
+        w_scales = keep.tile([P, PASSES, FEATURES], U8, align_bytes=64)
+
+        w_grouped_of = {}
+
+        def regroup_w(h):
+            turned = turn(wq_sb[:, h, :], evens_first)
+            w_grouped = work.tile([P, PASSES * HEAD_DIM * PACK], BF16, align_bytes=64)
+            words = w_grouped[:].bitcast(F32).rearrange("p (g r u) -> p g r u", g=PASSES, u=HALVES)
+            if h % 2 == 0:
+                nc.scalar.copy(out=words, in_=by_packed_word(turned))
+            else:
+                nc.vector.tensor_copy(out=words, in_=by_packed_word(turned))
+            w_grouped_of[h] = w_grouped
+
+        def quantise_w(h):
+            features = slice(h * HEAD_DIM, (h + 1) * HEAD_DIM)
+            for g in range(PASSES):
+                nc.vector.quantize_mx(
+                    out=w_codes[:, g, features].bitcast(FP8X4),
+                    scales=w_scales[:, g, features],
+                    in_=w_grouped_of[h][:, g * HEAD_DIM * PACK : (g + 1) * HEAD_DIM * PACK],
+                )
+
+        for h in range(HEADS + 1):
+            if h < HEADS:
+                regroup_w(h)
+            if h > 0:
+                quantise_w(h - 1)
+
+        turned_of, grouped_of, codes_of, scales_of = {}, {}, {}, {}
+        q_of, squares_of, inverse_of = {}, {}, {}
+
+        def transpose_x(n):
+            turned_of[n] = turn(x_sb[:, n, :], identity)
+
+        def regroup_x(n):
+            x_grouped = stage.tile([P, PASSES * P * PACK], BF16, align_bytes=64)
+            nc.scalar.copy(
+                out=x_grouped[:].bitcast(F32).rearrange("p (g r u) -> p g r u", g=PASSES, u=HALVES),
+                in_=by_packed_word(turned_of[n]),
+            )
+            grouped_of[n] = x_grouped
+
+        def quantise_x(n):
+            x_codes = stage.tile([P, PASSES * P], U32, align_bytes=64)
+            x_scales = stage.tile([P, PASSES * P], U8, align_bytes=64)
+            nc.vector.quantize_mx(out=x_codes[:].bitcast(FP8X4), scales=x_scales[:], in_=grouped_of[n][:])
+            codes_of[n], scales_of[n] = x_codes, x_scales
+
+        def multiply(n):
+            x_codes, x_scales = codes_of[n], scales_of[n]
+            q_of[n] = []
+            for b in range(BANKS):
+                q_bank = psum_q.tile([P, BANK], F32)
+                features = slice(b * BANK, (b + 1) * BANK)
+                for g in range(PASSES):
+                    tokens = slice(g * P, (g + 1) * P)
+                    nc.tensor.matmul_mx(
+                        out=q_bank[:],
+                        lhsT=x_codes[:, tokens].bitcast(FP8X4),
+                        lhsT_scale=x_scales[:, tokens],
+                        rhs=w_codes[:, g, features].bitcast(FP8X4),
+                        rhs_scale=w_scales[:, g, features],
+                        start=(g == 0),
+                        stop=(g == PASSES - 1),
+                    )
+                q_of[n].append(q_bank)
+
+        def head(n, h):
+            column = (h % HEADS_PER_BANK) * HEAD_DIM
+            return q_of[n][h // HEADS_PER_BANK][:, column : column + HEAD_DIM]
+
+        def bank_columns(products, h):
+            column = (h % HEADS_PER_BANK) * HEAD_DIM
+            return products[:, h // HEADS_PER_BANK, :, column : column + HEAD_DIM]
+
+        def sum_squares(n):
+            squares = stage.tile([P, HEADS], F32)
+            unread = stage.tile([P, FEATURES], BF16)
+            for h in range(HEADS):
+                nc.scalar.activation(
+                    out=unread[:, h * HEAD_DIM : (h + 1) * HEAD_DIM],
+                    in_=head(n, h),
+                    func=ACT.Square,
+                    accum_out=squares[:, h : h + 1],
+                )
+            squares_of[n] = squares
+
+        def inverse_rms(n, b):
+            if b == 0:
+                inverse = stage.tile([P, HEADS], F32)
+                inverse_of[n] = inverse
+            heads = slice(b * HEADS_PER_BANK, (b + 1) * HEADS_PER_BANK)
+            nc.scalar.activation(
+                out=inverse_of[n][:, heads],
+                in_=squares_of[n][:, heads],
+                func=ACT.Abs_reciprocal_sqrt,
+                scale=1.0 / HEAD_DIM,
+                bias=eps[:],
+            )
+
+        def inverse_rms_first_bank(n):
+            inverse_rms(n, 0)
+
+        def inverse_rms_second_bank(n):
+            inverse_rms(n, 1)
+
+        def rotate(n):
+            inverse = inverse_of[n]
+            products = work.tile([P, BANKS, 2, BANK], F32)
+
+            def add_and_store(adder, first_bank, banks):
+                some = slice(first_bank, first_bank + banks)
+                rotated = results.tile([P, banks, BANK], F32)
+                adder.tensor_tensor(out=rotated[:], in0=products[:, some, 0, :], in1=products[:, some, 1, :], op=ALU.add)
+                first = n - n % GROUP
+                out_group = out_rows[first * P : (first + GROUP) * P, :].rearrange("(p i) (b f) -> p i b f", i=GROUP, f=BANK)
+                nc.sync.dma_start(out=out_group[:, n % GROUP, some, :], in_=rotated[:])
+
+            for h in range(HEADS):
+                nc.vector.scalar_tensor_tensor(
+                    out=bank_columns(products, h).rearrange("p a (j e) -> p a j e", e=2),
+                    in0=head(n, h).rearrange("p (a j) -> p a j", a=2).unsqueeze(3).to_broadcast([P, 2, PAIRS, 2]),
+                    scalar=inverse[:, h : h + 1],
+                    in1=rot[:, n % TABLES, :].rearrange("p (a j e) -> p a j e", a=2, e=2),
+                    op0=ALU.mult,
+                    op1=ALU.mult,
+                )
+            if n < TILES - 1:
+                add_and_store(nc.gpsimd, 0, BANKS)
+            else:
+                for b in range(BANKS):
+                    add_and_store(nc.vector, b, 1)
+
+        def when_valid(stage_of_tile, n):
+            if 0 <= n < TILES:
+                stage_of_tile(n)
+
+        for step in range(-4, TILES):
+            when_valid(quantise_x, step + 2)
+            when_valid(multiply, step + 2)
+            when_valid(transpose_x, step + 4)
+            when_valid(sum_squares, step + 1)
+            when_valid(inverse_rms_first_bank, step + 1)
+            when_valid(regroup_x, step + 3)
+            when_valid(inverse_rms_second_bank, step + 1)
+            when_valid(rotate, step)

@@ -33,6 +33,12 @@ TILES = TOKENS // P
 TABLES = SEQUENCE // P
 
 FLOPS = 2 * TOKENS * K * FEATURES
+UNIT_HEADS = 2
+UNITS = HEADS // UNIT_HEADS
+UNIT = UNIT_HEADS * HEAD_DIM
+EARLY_TILES = 2
+AHEAD = 4
+LOADED_AHEAD = 3
 
 
 def tile_mla_pb_t_kernel(tc, x, wq, q_norm_w, freqs_cos, freqs_sin, out):
@@ -42,7 +48,7 @@ def tile_mla_pb_t_kernel(tc, x, wq, q_norm_w, freqs_cos, freqs_sin, out):
 
     with ExitStack() as stack:
         keep = stack.enter_context(tc.tile_pool(name="keep", bufs=1))
-        stage = stack.enter_context(tc.tile_pool(name="stage", bufs=2))
+        stage = stack.enter_context(tc.tile_pool(name="stage", bufs=3))
         work = stack.enter_context(tc.tile_pool(name="work", bufs=3))
         results = stack.enter_context(tc.tile_pool(name="results", bufs=4))
         psum_turned = stack.enter_context(tc.psum_pool(name="psum_turned", bufs=2))
@@ -52,23 +58,34 @@ def tile_mla_pb_t_kernel(tc, x, wq, q_norm_w, freqs_cos, freqs_sin, out):
         gain_row = keep.tile([P, HEAD_DIM], BF16)
         nc.vector.memset(gain_row[:], 0.0)
         nc.sync.dma_start(out=gain_row[0:1, :], in_=q_norm_w.unsqueeze(0))
-        cos = keep.tile([P, TABLES // GROUP, GROUP * PAIRS], BF16)
-        sin = keep.tile([P, TABLES // GROUP, GROUP * PAIRS], BF16)
-        for table, freqs in ((cos, freqs_cos), (sin, freqs_sin)):
-            nc.scalar.dma_start(out=table[:], in_=freqs.rearrange("(s p i) j -> p s (i j)", p=P, i=GROUP))
-
+        trig = keep.tile([P, 3, TABLES * PAIRS], BF16)
+        for k, freqs in ((1, freqs_cos), (2, freqs_sin)):
+            nc.scalar.dma_start(
+                out=trig[:, k, :].rearrange("p (s r) -> p s r", r=GROUP * PAIRS),
+                in_=freqs.rearrange("(s p i) j -> p s (i j)", p=P, i=GROUP),
+            )
         wq_sb = keep.tile([P, HEADS, K], BF16)
         wq_by_head = wq.rearrange("(h p) k -> p h k", p=P)
+        x_sb = keep.tile([P, TILES, K], BF16)
+
+        def group_rows(group):
+            first = group * GROUP
+            return x_rows[first * P : (first + GROUP) * P, :].rearrange("(p i) k -> p i k", i=GROUP)
+
+        def load_x_tile(n):
+            nc.sync.dma_start(out=x_sb[:, n, :], in_=group_rows(n // GROUP)[:, n % GROUP, :])
+
+        def load_x_group(group):
+            nc.sync.dma_start(out=x_sb[:, group * GROUP : (group + 1) * GROUP, :], in_=group_rows(group))
+
         for h in range(HEADS):
             nc.sync.dma_start(out=wq_sb[:, h, :], in_=wq_by_head[:, h, :])
-        x_sb = keep.tile([P, TILES, K], BF16)
-        for first in range(0, TILES, GROUP):
-            x_group = x_rows[first * P : (first + GROUP) * P, :].rearrange("(p i) k -> p i k", i=GROUP)
-            if first == 0:
-                for i in range(GROUP):
-                    nc.sync.dma_start(out=x_sb[:, i, :], in_=x_group[:, i, :])
-            else:
-                nc.sync.dma_start(out=x_sb[:, first : first + GROUP, :], in_=x_group)
+            if h < EARLY_TILES:
+                load_x_tile(h)
+        for n in range(EARLY_TILES, GROUP):
+            load_x_tile(n)
+        for group in range(1, LOADED_AHEAD):
+            load_x_group(group)
 
         eps = keep.tile([P, 1], F32)
         nc.vector.memset(eps[:], EPS)
@@ -85,23 +102,25 @@ def tile_mla_pb_t_kernel(tc, x, wq, q_norm_w, freqs_cos, freqs_sin, out):
 
         ones = keep.tile([P, P], BF16)
         nc.vector.memset(ones[:], 1.0)
-        gain_bank = psum_turned.tile([P, WORD_BLOCKS, P], F32, tag="turned")
-        nc.tensor.matmul(out=gain_bank[:, 0, :], lhsT=ones[:], rhs=gain_row[:], start=True, stop=True)
+        gain_bank = psum_q.tile([P, BANK], F32, tag="q_bank")
+        nc.tensor.matmul(out=gain_bank[:, :HEAD_DIM], lhsT=ones[:], rhs=gain_row[:], start=True, stop=True)
         gain = keep.tile([P, HEAD_DIM], F32)
-        nc.vector.tensor_copy(out=gain[:], in_=gain_bank[:, 0, :])
+        nc.vector.tensor_copy(out=gain[:], in_=gain_bank[:, :HEAD_DIM])
+        nc.vector.tensor_scalar(out=trig[:, 0, :], in0=trig[:, 2, :], scalar1=-1.0, scalar2=None, op0=ALU.mult)
 
-        neg_sin = keep.tile([P, TABLES // GROUP, GROUP * PAIRS], BF16)
-        nc.gpsimd.tensor_scalar(out=neg_sin[:], in0=sin[:], scalar1=-1.0, scalar2=0.0, op0=ALU.mult, op1=ALU.add)
         rot = keep.tile([P, TABLES, 2 * HEAD_DIM], F32)
-        rot_parts = rot[:].rearrange("p m (a j e) -> p e a m j", a=2, e=2)
         gain_parts = gain[:].rearrange("p (j a) -> p a j", a=2)
-        for e, a, trig in ((0, 0, cos), (0, 1, neg_sin), (1, 0, sin), (1, 1, cos)):
-            nc.gpsimd.tensor_tensor(
-                out=rot_parts[:, e, a],
-                in0=trig[:].rearrange("p s (i j) -> p (s i) j", i=GROUP),
-                in1=gain_parts[:, a].unsqueeze(1).to_broadcast([P, TABLES, PAIRS]),
-                op=ALU.mult,
-            )
+
+        def make_tables(first, last):
+            for a in range(2):
+                nc.vector.tensor_tensor(
+                    out=rot[:, first:last, a * HEAD_DIM : (a + 1) * HEAD_DIM].rearrange("p m (j e) -> p m j e", e=2),
+                    in0=trig[:, 1 - a : 3 - a, first * PAIRS : last * PAIRS].rearrange("p e (m j) -> p m j e", j=PAIRS),
+                    in1=gain_parts[:, a].unsqueeze(1).unsqueeze(3).to_broadcast([P, last - first, PAIRS, 2]),
+                    op=ALU.mult,
+                )
+
+        make_tables(0, GROUP)
 
         def turn(rows, selector):
             turned = psum_turned.tile([P, WORD_BLOCKS, P], F32)
@@ -112,51 +131,40 @@ def tile_mla_pb_t_kernel(tc, x, wq, q_norm_w, freqs_cos, freqs_sin, out):
                     nc.tensor.transpose(turned[:, g * HALVES + u, :], words[:, first + u : last : HALVES], selector[:])
             return turned
 
-        def by_packed_word(turned):
-            return turned[:].rearrange("p (g u) r -> p g r u", u=HALVES)
+        def regroup(copy, grouped, turned):
+            copy(out=grouped, in_=turned[:].rearrange("p (g u) r -> p g r u", u=HALVES))
 
-        w_codes = keep.tile([P, PASSES, FEATURES], U32, align_bytes=64)
-        w_scales = keep.tile([P, PASSES, FEATURES], U8, align_bytes=64)
+        w_codes = keep.tile([P, UNITS, PASSES, UNIT], U32, align_bytes=64)
+        w_scales = keep.tile([P, UNITS, PASSES, UNIT], U8, align_bytes=64)
+        w_turned_of, w_grouped_of = {}, {}
 
-        w_grouped_of = {}
+        def transpose_w(h):
+            w_turned_of[h] = turn(wq_sb[:, h, :], evens_first)
 
         def regroup_w(h):
-            turned = turn(wq_sb[:, h, :], evens_first)
-            w_grouped = work.tile([P, PASSES * HEAD_DIM * PACK], BF16, align_bytes=64)
-            words = w_grouped[:].bitcast(F32).rearrange("p (g r u) -> p g r u", g=PASSES, u=HALVES)
-            if h % 2 == 0:
-                nc.scalar.copy(out=words, in_=by_packed_word(turned))
-            else:
-                nc.vector.tensor_copy(out=words, in_=by_packed_word(turned))
-            w_grouped_of[h] = w_grouped
+            if h % UNIT_HEADS == 0:
+                w_grouped = work.tile([P, PASSES * UNIT * PACK], BF16, align_bytes=64)
+                w_grouped_of[h // UNIT_HEADS] = w_grouped
+            words = w_grouped_of[h // UNIT_HEADS][:].bitcast(F32)
+            by_head = words.rearrange("p (g i r u) -> p g i r u", g=PASSES, i=UNIT_HEADS, u=HALVES)
+            regroup(nc.scalar.copy, by_head[:, :, h % UNIT_HEADS], w_turned_of[h])
 
-        def quantise_w(h):
-            features = slice(h * HEAD_DIM, (h + 1) * HEAD_DIM)
-            for g in range(PASSES):
-                nc.vector.quantize_mx(
-                    out=w_codes[:, g, features].bitcast(FP8X4),
-                    scales=w_scales[:, g, features],
-                    in_=w_grouped_of[h][:, g * HEAD_DIM * PACK : (g + 1) * HEAD_DIM * PACK],
-                )
-
-        for h in range(HEADS + 1):
-            if h < HEADS:
-                regroup_w(h)
-            if h > 0:
-                quantise_w(h - 1)
+        def quantise_w(unit):
+            nc.vector.quantize_mx(
+                out=w_codes[:, unit, :, :].rearrange("p g f -> p (g f)").bitcast(FP8X4),
+                scales=w_scales[:, unit, :, :].rearrange("p g f -> p (g f)"),
+                in_=w_grouped_of[unit][:],
+            )
 
         turned_of, grouped_of, codes_of, scales_of = {}, {}, {}, {}
-        q_of, squares_of, inverse_of = {}, {}, {}
 
         def transpose_x(n):
             turned_of[n] = turn(x_sb[:, n, :], identity)
 
         def regroup_x(n):
             x_grouped = stage.tile([P, PASSES * P * PACK], BF16, align_bytes=64)
-            nc.scalar.copy(
-                out=x_grouped[:].bitcast(F32).rearrange("p (g r u) -> p g r u", g=PASSES, u=HALVES),
-                in_=by_packed_word(turned_of[n]),
-            )
+            words = x_grouped[:].bitcast(F32).rearrange("p (g r u) -> p g r u", g=PASSES, u=HALVES)
+            regroup(nc.scalar.copy, words, turned_of[n])
             grouped_of[n] = x_grouped
 
         def quantise_x(n):
@@ -165,84 +173,122 @@ def tile_mla_pb_t_kernel(tc, x, wq, q_norm_w, freqs_cos, freqs_sin, out):
             nc.vector.quantize_mx(out=x_codes[:].bitcast(FP8X4), scales=x_scales[:], in_=grouped_of[n][:])
             codes_of[n], scales_of[n] = x_codes, x_scales
 
-        def multiply(n):
-            x_codes, x_scales = codes_of[n], scales_of[n]
-            q_of[n] = []
-            for b in range(BANKS):
-                q_bank = psum_q.tile([P, BANK], F32)
-                features = slice(b * BANK, (b + 1) * BANK)
-                for g in range(PASSES):
-                    tokens = slice(g * P, (g + 1) * P)
-                    nc.tensor.matmul_mx(
-                        out=q_bank[:],
-                        lhsT=x_codes[:, tokens].bitcast(FP8X4),
-                        lhsT_scale=x_scales[:, tokens],
-                        rhs=w_codes[:, g, features].bitcast(FP8X4),
-                        rhs_scale=w_scales[:, g, features],
-                        start=(g == 0),
-                        stop=(g == PASSES - 1),
-                    )
-                q_of[n].append(q_bank)
+        q_of, squares_of, inverse_of = {}, {}, {}
 
-        def head(n, h):
-            column = (h % HEADS_PER_BANK) * HEAD_DIM
-            return q_of[n][h // HEADS_PER_BANK][:, column : column + HEAD_DIM]
-
-        def bank_columns(products, h):
-            column = (h % HEADS_PER_BANK) * HEAD_DIM
-            return products[:, h // HEADS_PER_BANK, :, column : column + HEAD_DIM]
-
-        def sum_squares(n):
-            squares = stage.tile([P, HEADS], F32)
-            unread = stage.tile([P, FEATURES], BF16)
-            for h in range(HEADS):
-                nc.scalar.activation(
-                    out=unread[:, h * HEAD_DIM : (h + 1) * HEAD_DIM],
-                    in_=head(n, h),
-                    func=ACT.Square,
-                    accum_out=squares[:, h : h + 1],
+        def multiply(n, unit, q):
+            for g in range(PASSES):
+                tokens = slice(g * P, (g + 1) * P)
+                nc.tensor.matmul_mx(
+                    out=q,
+                    lhsT=codes_of[n][:, tokens].bitcast(FP8X4),
+                    lhsT_scale=scales_of[n][:, tokens],
+                    rhs=w_codes[:, unit, g, :].bitcast(FP8X4),
+                    rhs_scale=w_scales[:, unit, g, :],
+                    start=(g == 0),
+                    stop=(g == PASSES - 1),
                 )
-            squares_of[n] = squares
+            q_of[n, unit] = q
 
-        def inverse_rms(n, b):
+        def multiply_early(unit):
+            for n in range(EARLY_TILES):
+                q_bank = psum_q.tile([P, BANK], F32, tag="q_bank")
+                multiply(n, unit, q_bank[:, :UNIT])
+
+        def multiply_tile(n):
+            for b in range(BANKS):
+                q_bank = psum_q.tile([P, BANK], F32, tag="q_bank")
+                for part in range(BANK // UNIT):
+                    multiply(n, b * BANK // UNIT + part, q_bank[:, part * UNIT : (part + 1) * UNIT])
+
+        def head_columns(i):
+            return slice(i * HEAD_DIM, (i + 1) * HEAD_DIM)
+
+        def square_unit(n, unit, sums):
+            unread = stage.tile([P, UNIT], BF16)
+            for i in range(UNIT_HEADS):
+                nc.scalar.activation(
+                    out=unread[:, head_columns(i)],
+                    in_=q_of[n, unit][:, head_columns(i)],
+                    func=ACT.Square,
+                    accum_out=sums[:, i : i + 1],
+                )
+
+        def invert_rms(inverse, squares):
+            nc.scalar.activation(out=inverse, in_=squares, func=ACT.Abs_reciprocal_sqrt, scale=1.0 / HEAD_DIM, bias=eps[:])
+
+        def square_early(unit):
+            squares = stage.tile([P, EARLY_TILES * UNIT_HEADS], F32, tag="early_squares")
+            for n in range(EARLY_TILES):
+                square_unit(n, unit, squares[:, n * UNIT_HEADS : (n + 1) * UNIT_HEADS])
+            squares_of[unit] = squares
+
+        def invert_early(unit):
+            inverse = stage.tile([P, EARLY_TILES * UNIT_HEADS], F32, tag="early_inverse")
+            invert_rms(inverse[:], squares_of[unit][:])
+            inverse_of[unit] = inverse
+
+        def square_tile(n):
+            squares = stage.tile([P, HEADS], F32)
+            for unit in range(UNITS):
+                square_unit(n, unit, squares[:, unit * UNIT_HEADS : (unit + 1) * UNIT_HEADS])
+            squares_of["tile", n] = squares
+
+        def invert_bank(n, b):
             if b == 0:
                 inverse = stage.tile([P, HEADS], F32)
-                inverse_of[n] = inverse
+                inverse_of["tile", n] = inverse
             heads = slice(b * HEADS_PER_BANK, (b + 1) * HEADS_PER_BANK)
-            nc.scalar.activation(
-                out=inverse_of[n][:, heads],
-                in_=squares_of[n][:, heads],
-                func=ACT.Abs_reciprocal_sqrt,
-                scale=1.0 / HEAD_DIM,
-                bias=eps[:],
+            invert_rms(inverse_of["tile", n][:, heads], squares_of["tile", n][:, heads])
+
+        def multiply_by_table(n, q, inverse, products):
+            nc.vector.scalar_tensor_tensor(
+                out=products.rearrange("p a (j e) -> p a j e", e=2),
+                in0=q.rearrange("p (a j) -> p a j", a=2).unsqueeze(3).to_broadcast([P, 2, PAIRS, 2]),
+                scalar=inverse,
+                in1=rot[:, n % TABLES, :].rearrange("p (a j e) -> p a j e", a=2, e=2),
+                op0=ALU.mult,
+                op1=ALU.mult,
             )
 
-        def inverse_rms_first_bank(n):
-            inverse_rms(n, 0)
+        def store(n, columns, rotated):
+            nc.sync.dma_start(
+                out=out_rows[n // GROUP * GROUP * P : (n // GROUP + 1) * GROUP * P, columns].rearrange("(p i) f -> p i f", i=GROUP)[
+                    :, n % GROUP, :
+                ],
+                in_=rotated,
+            )
 
-        def inverse_rms_second_bank(n):
-            inverse_rms(n, 1)
+        def rotate_early(unit):
+            products = work.tile([P, EARLY_TILES, 2, UNIT], F32, tag="early_products")
+            for n in range(EARLY_TILES):
+                for i in range(UNIT_HEADS):
+                    column = n * UNIT_HEADS + i
+                    multiply_by_table(
+                        n,
+                        q_of[n, unit][:, head_columns(i)],
+                        inverse_of[unit][:, column : column + 1],
+                        products[:, n, :, head_columns(i)],
+                    )
+            rotated = results.tile([P, EARLY_TILES, UNIT], F32, tag="early_rotated")
+            nc.gpsimd.tensor_tensor(out=rotated[:], in0=products[:, :, 0, :], in1=products[:, :, 1, :], op=ALU.add)
+            for n in range(EARLY_TILES):
+                store(n, slice(unit * UNIT, (unit + 1) * UNIT), rotated[:, n, :])
 
-        def rotate(n):
-            inverse = inverse_of[n]
+        def rotate_tile(n):
             products = work.tile([P, BANKS, 2, BANK], F32)
 
             def add_and_store(adder, first_bank, banks):
                 some = slice(first_bank, first_bank + banks)
                 rotated = results.tile([P, banks, BANK], F32)
                 adder.tensor_tensor(out=rotated[:], in0=products[:, some, 0, :], in1=products[:, some, 1, :], op=ALU.add)
-                first = n - n % GROUP
-                out_group = out_rows[first * P : (first + GROUP) * P, :].rearrange("(p i) (b f) -> p i b f", i=GROUP, f=BANK)
-                nc.sync.dma_start(out=out_group[:, n % GROUP, some, :], in_=rotated[:])
+                store(n, slice(first_bank * BANK, (first_bank + banks) * BANK), rotated[:].rearrange("p b f -> p (b f)"))
 
             for h in range(HEADS):
-                nc.vector.scalar_tensor_tensor(
-                    out=bank_columns(products, h).rearrange("p a (j e) -> p a j e", e=2),
-                    in0=head(n, h).rearrange("p (a j) -> p a j", a=2).unsqueeze(3).to_broadcast([P, 2, PAIRS, 2]),
-                    scalar=inverse[:, h : h + 1],
-                    in1=rot[:, n % TABLES, :].rearrange("p (a j e) -> p a j e", a=2, e=2),
-                    op0=ALU.mult,
-                    op1=ALU.mult,
+                multiply_by_table(
+                    n,
+                    q_of[n, h // UNIT_HEADS][:, head_columns(h % UNIT_HEADS)],
+                    inverse_of["tile", n][:, h : h + 1],
+                    products[:, h // HEADS_PER_BANK, :, head_columns(h % HEADS_PER_BANK)],
                 )
             if n < TILES - 1:
                 add_and_store(nc.gpsimd, 0, BANKS)
@@ -250,16 +296,63 @@ def tile_mla_pb_t_kernel(tc, x, wq, q_norm_w, freqs_cos, freqs_sin, out):
                 for b in range(BANKS):
                     add_and_store(nc.vector, b, 1)
 
-        def when_valid(stage_of_tile, n):
-            if 0 <= n < TILES:
-                stage_of_tile(n)
+        def when_valid(stage_of_item, item, first, end):
+            if first <= item < end:
+                stage_of_item(item)
 
-        for step in range(-4, TILES):
-            when_valid(quantise_x, step + 2)
-            when_valid(multiply, step + 2)
-            when_valid(transpose_x, step + 4)
-            when_valid(sum_squares, step + 1)
-            when_valid(inverse_rms_first_bank, step + 1)
-            when_valid(regroup_x, step + 3)
-            when_valid(inverse_rms_second_bank, step + 1)
-            when_valid(rotate, step)
+        items = []
+        for h in range(HEADS):
+            items.append((transpose_w, regroup_w, h))
+            if h < EARLY_TILES:
+                items.append((transpose_x, regroup_x, h))
+        for n in range(EARLY_TILES, TILES):
+            items.append((transpose_x, regroup_x, n))
+
+        def transpose_item(i):
+            items[i][0](items[i][2])
+
+        def regroup_item(i):
+            items[i][1](items[i][2])
+
+        done = 0
+        transpose_item(0)
+        for step in range(-3, UNITS):
+            last = done + (UNIT_HEADS + EARLY_TILES if step == -3 else UNIT_HEADS if step < 1 else 1)
+            for i in range(done, last):
+                transpose_item(i + 1)
+                regroup_item(i)
+                if i == done:
+                    when_valid(multiply_early, step + 1, 0, UNITS)
+                    when_valid(square_early, step + 1, 0, UNITS)
+            when_valid(invert_early, step + 1, 0, UNITS)
+            if step == UNITS - 1:
+                for n in range(EARLY_TILES, EARLY_TILES + 2):
+                    multiply_tile(n)
+                square_tile(EARLY_TILES)
+                for b in range(BANKS):
+                    invert_bank(EARLY_TILES, b)
+            done = last
+            when_valid(rotate_early, step, 0, UNITS)
+            when_valid(quantise_w, step + 2, 0, UNITS)
+            if step == -2:
+                for n in range(EARLY_TILES):
+                    quantise_x(n)
+            if step == -1:
+                make_tables(GROUP, TABLES)
+            when_valid(quantise_x, step + 1, EARLY_TILES, EARLY_TILES + 2)
+
+
+        for step in range(EARLY_TILES, TILES):
+            group = LOADED_AHEAD + (step - EARLY_TILES) // GROUP
+            if (step - EARLY_TILES) % GROUP == 0 and group < TILES // GROUP:
+                load_x_group(group)
+            when_valid(quantise_x, step + 2, 0, TILES)
+            when_valid(multiply_tile, step + 2, 0, TILES)
+            when_valid(transpose_x, step + AHEAD, 0, TILES)
+            when_valid(square_tile, step + 1, 0, TILES)
+            if step + 1 < TILES:
+                invert_bank(step + 1, 0)
+            when_valid(regroup_x, step + 3, 0, TILES)
+            if step + 1 < TILES:
+                invert_bank(step + 1, 1)
+            rotate_tile(step)

@@ -51,8 +51,8 @@ def tile_mla_pb_t_kernel(tc, x, wq, q_norm_w, freqs_cos, freqs_sin, out):
         stage = stack.enter_context(tc.tile_pool(name="stage", bufs=3))
         work = stack.enter_context(tc.tile_pool(name="work", bufs=3))
         results = stack.enter_context(tc.tile_pool(name="results", bufs=4))
-        psum_turned = stack.enter_context(tc.psum_pool(name="psum_turned", bufs=2))
-        psum_q = stack.enter_context(tc.psum_pool(name="psum_q", bufs=3 * BANKS))
+        psum_turned = stack.enter_context(tc.psum_pool(name="psum_turned", bufs=3))
+        psum_q = stack.enter_context(tc.psum_pool(name="psum_q", bufs=5))
         stack.enter_context(tc.manual_schedule())
 
         gain_row = keep.tile([P, HEAD_DIM], BF16)
@@ -147,7 +147,7 @@ def tile_mla_pb_t_kernel(tc, x, wq, q_norm_w, freqs_cos, freqs_sin, out):
                 w_grouped_of[h // UNIT_HEADS] = w_grouped
             words = w_grouped_of[h // UNIT_HEADS][:].bitcast(F32)
             by_head = words.rearrange("p (g i r u) -> p g i r u", g=PASSES, i=UNIT_HEADS, u=HALVES)
-            regroup(nc.scalar.copy, by_head[:, :, h % UNIT_HEADS], w_turned_of[h])
+            regroup(nc.vector.tensor_copy if h in (4,) else nc.scalar.copy, by_head[:, :, h % UNIT_HEADS], w_turned_of[h])
 
         def quantise_w(unit):
             nc.vector.quantize_mx(
@@ -194,11 +194,10 @@ def tile_mla_pb_t_kernel(tc, x, wq, q_norm_w, freqs_cos, freqs_sin, out):
                 q_bank = psum_q.tile([P, BANK], F32, tag="q_bank")
                 multiply(n, unit, q_bank[:, :UNIT])
 
-        def multiply_tile(n):
-            for b in range(BANKS):
-                q_bank = psum_q.tile([P, BANK], F32, tag="q_bank")
-                for part in range(BANK // UNIT):
-                    multiply(n, b * BANK // UNIT + part, q_bank[:, part * UNIT : (part + 1) * UNIT])
+        def multiply_bank(n, b):
+            q_bank = psum_q.tile([P, BANK], F32, tag="q_bank")
+            for part in range(BANK // UNIT):
+                multiply(n, b * BANK // UNIT + part, q_bank[:, part * UNIT : (part + 1) * UNIT])
 
         def head_columns(i):
             return slice(i * HEAD_DIM, (i + 1) * HEAD_DIM)
@@ -274,7 +273,7 @@ def tile_mla_pb_t_kernel(tc, x, wq, q_norm_w, freqs_cos, freqs_sin, out):
             for n in range(EARLY_TILES):
                 store(n, slice(unit * UNIT, (unit + 1) * UNIT), rotated[:, n, :])
 
-        def rotate_tile(n):
+        def rotate_tile(n, between_banks):
             products = work.tile([P, BANKS, 2, BANK], F32)
 
             def add_and_store(adder, first_bank, banks):
@@ -284,6 +283,8 @@ def tile_mla_pb_t_kernel(tc, x, wq, q_norm_w, freqs_cos, freqs_sin, out):
                 store(n, slice(first_bank * BANK, (first_bank + banks) * BANK), rotated[:].rearrange("p b f -> p (b f)"))
 
             for h in range(HEADS):
+                if h == HEADS_PER_BANK:
+                    between_banks()
                 multiply_by_table(
                     n,
                     q_of[n, h // UNIT_HEADS][:, head_columns(h % UNIT_HEADS)],
@@ -314,32 +315,40 @@ def tile_mla_pb_t_kernel(tc, x, wq, q_norm_w, freqs_cos, freqs_sin, out):
         def regroup_item(i):
             items[i][1](items[i][2])
 
-        done = 0
+        rotations = {8: 0, 10: 1, 11: 2, 12: 3}
+        squares = {6: 0, 8: 1, 10: 2, 11: 3}
         transpose_item(0)
-        for step in range(-3, UNITS):
-            last = done + (UNIT_HEADS + EARLY_TILES if step == -3 else UNIT_HEADS if step < 1 else 1)
-            for i in range(done, last):
-                transpose_item(i + 1)
-                regroup_item(i)
-                if i == done:
-                    when_valid(multiply_early, step + 1, 0, UNITS)
-                    when_valid(square_early, step + 1, 0, UNITS)
-            when_valid(invert_early, step + 1, 0, UNITS)
-            if step == UNITS - 1:
-                for n in range(EARLY_TILES, EARLY_TILES + 2):
-                    multiply_tile(n)
+        for step in range(13):
+            if step % 2 == 0 and 4 <= step <= 10:
+                quantise_w((step - 4) // 2)
+            if step == 4:
+                for n in range(EARLY_TILES):
+                    quantise_x(n)
+            if step >= 11:
+                quantise_x(step - 9)
+            if step in (5, 7):
+                multiply_early((step - 5) // 2)
+            if step in squares:
+                square_early(squares[step])
+                invert_early(squares[step])
+            if step == 12:
                 square_tile(EARLY_TILES)
                 for b in range(BANKS):
                     invert_bank(EARLY_TILES, b)
-            done = last
-            when_valid(rotate_early, step, 0, UNITS)
-            when_valid(quantise_w, step + 2, 0, UNITS)
-            if step == -2:
-                for n in range(EARLY_TILES):
-                    quantise_x(n)
-            if step == -1:
+            transpose_item(step + 1)
+            regroup_item(step)
+            if step in rotations:
+                rotate_early(rotations[step])
+                if rotations[step] < 2:
+                    multiply_early(rotations[step] + 2)
+            if step == 11:
+                multiply_bank(EARLY_TILES, 0)
+                multiply_bank(EARLY_TILES, 1)
+            if step == 12:
+                multiply_bank(EARLY_TILES + 1, 0)
+                multiply_bank(EARLY_TILES + 1, 1)
+            if step == 7:
                 make_tables(GROUP, TABLES)
-            when_valid(quantise_x, step + 1, EARLY_TILES, EARLY_TILES + 2)
 
 
         for step in range(EARLY_TILES, TILES):
@@ -347,7 +356,8 @@ def tile_mla_pb_t_kernel(tc, x, wq, q_norm_w, freqs_cos, freqs_sin, out):
             if (step - EARLY_TILES) % GROUP == 0 and group < TILES // GROUP:
                 load_x_group(group)
             when_valid(quantise_x, step + 2, 0, TILES)
-            when_valid(multiply_tile, step + 2, 0, TILES)
+            if step + 2 < TILES:
+                multiply_bank(step + 2, 0)
             when_valid(transpose_x, step + AHEAD, 0, TILES)
             when_valid(square_tile, step + 1, 0, TILES)
             if step + 1 < TILES:
@@ -355,4 +365,4 @@ def tile_mla_pb_t_kernel(tc, x, wq, q_norm_w, freqs_cos, freqs_sin, out):
             when_valid(regroup_x, step + 3, 0, TILES)
             if step + 1 < TILES:
                 invert_bank(step + 1, 1)
-            rotate_tile(step)
+            rotate_tile(step, lambda n=step + 2: multiply_bank(n, 1) if n < TILES else None)

@@ -57,13 +57,14 @@ def tile_mla_pb_t_kernel(tc, x, wq, q_norm_w, freqs_cos, freqs_sin, out):
 
         gain_row = keep.tile([P, HEAD_DIM], BF16)
         nc.vector.memset(gain_row[:], 0.0)
-        nc.sync.dma_start(out=gain_row[0:1, :], in_=q_norm_w.unsqueeze(0))
         trig = keep.tile([P, 3, TABLES * PAIRS], BF16)
-        for k, freqs in ((1, freqs_cos), (2, freqs_sin)):
-            nc.scalar.dma_start(
-                out=trig[:, k, :].rearrange("p (s r) -> p s r", r=GROUP * PAIRS),
-                in_=freqs.rearrange("(s p i) j -> p s (i j)", p=P, i=GROUP),
-            )
+
+        def load_trig(queue, s):
+            columns = slice(s * GROUP * PAIRS, (s + 1) * GROUP * PAIRS)
+            for k, freqs in ((1, freqs_cos), (2, freqs_sin)):
+                queue.dma_start(out=trig[:, k, columns], in_=freqs[s * GROUP * P : (s + 1) * GROUP * P, :].rearrange("(p i) j -> p (i j)", i=GROUP))
+
+        load_trig(nc.scalar, 0)
         wq_sb = keep.tile([P, HEADS, K], BF16)
         wq_by_head = wq.rearrange("(h p) k -> p h k", p=P)
         x_sb = keep.tile([P, TILES, K], BF16)
@@ -80,8 +81,12 @@ def tile_mla_pb_t_kernel(tc, x, wq, q_norm_w, freqs_cos, freqs_sin, out):
 
         for h in range(HEADS):
             nc.sync.dma_start(out=wq_sb[:, h, :], in_=wq_by_head[:, h, :])
+            if h == 0:
+                nc.sync.dma_start(out=gain_row[0:1, :], in_=q_norm_w.unsqueeze(0))
             if h < EARLY_TILES:
                 load_x_tile(h)
+            if h == 3:
+                load_trig(nc.sync, 1)
         for n in range(EARLY_TILES, GROUP):
             load_x_tile(n)
         for group in range(1, LOADED_AHEAD):
@@ -106,12 +111,13 @@ def tile_mla_pb_t_kernel(tc, x, wq, q_norm_w, freqs_cos, freqs_sin, out):
         nc.tensor.matmul(out=gain_bank[:, :HEAD_DIM], lhsT=ones[:], rhs=gain_row[:], start=True, stop=True)
         gain = keep.tile([P, HEAD_DIM], F32)
         nc.vector.tensor_copy(out=gain[:], in_=gain_bank[:, :HEAD_DIM])
-        nc.vector.tensor_scalar(out=trig[:, 0, :], in0=trig[:, 2, :], scalar1=-1.0, scalar2=None, op0=ALU.mult)
 
         rot = keep.tile([P, TABLES, 2 * HEAD_DIM], F32)
         gain_parts = gain[:].rearrange("p (j a) -> p a j", a=2)
 
         def make_tables(first, last):
+            columns = slice(first * PAIRS, last * PAIRS)
+            nc.vector.tensor_scalar(out=trig[:, 0, columns], in0=trig[:, 2, columns], scalar1=-1.0, scalar2=None, op0=ALU.mult)
             for a in range(2):
                 nc.vector.tensor_tensor(
                     out=rot[:, first:last, a * HEAD_DIM : (a + 1) * HEAD_DIM].rearrange("p m (j e) -> p m j e", e=2),
@@ -147,7 +153,7 @@ def tile_mla_pb_t_kernel(tc, x, wq, q_norm_w, freqs_cos, freqs_sin, out):
                 w_grouped_of[h // UNIT_HEADS] = w_grouped
             words = w_grouped_of[h // UNIT_HEADS][:].bitcast(F32)
             by_head = words.rearrange("p (g i r u) -> p g i r u", g=PASSES, i=UNIT_HEADS, u=HALVES)
-            regroup(nc.vector.tensor_copy if h in (4,) else nc.scalar.copy, by_head[:, :, h % UNIT_HEADS], w_turned_of[h])
+            regroup(nc.scalar.copy, by_head[:, :, h % UNIT_HEADS], w_turned_of[h])
 
         def quantise_w(unit):
             nc.vector.quantize_mx(
@@ -328,6 +334,9 @@ def tile_mla_pb_t_kernel(tc, x, wq, q_norm_w, freqs_cos, freqs_sin, out):
                 quantise_x(step - 9)
             if step in (5, 7):
                 multiply_early((step - 5) // 2)
+            if step >= 11:
+                transpose_item(step + 1)
+                regroup_item(step)
             if step in squares:
                 square_early(squares[step])
                 invert_early(squares[step])
@@ -335,8 +344,9 @@ def tile_mla_pb_t_kernel(tc, x, wq, q_norm_w, freqs_cos, freqs_sin, out):
                 square_tile(EARLY_TILES)
                 for b in range(BANKS):
                     invert_bank(EARLY_TILES, b)
-            transpose_item(step + 1)
-            regroup_item(step)
+            if step < 11:
+                transpose_item(step + 1)
+                regroup_item(step)
             if step in rotations:
                 rotate_early(rotations[step])
                 if rotations[step] < 2:

@@ -105,12 +105,15 @@ def tile_mla_pb_t_kernel(tc, x, wq, q_norm_w, freqs_cos, freqs_sin, out):
             in_=identity[:].rearrange("p (j a) -> p a j", a=2),
         )
 
-        ones = keep.tile([P, P], BF16)
-        nc.vector.memset(ones[:], 1.0)
-        gain_bank = psum_q.tile([P, BANK], F32, tag="q_bank")
-        nc.tensor.matmul(out=gain_bank[:, :HEAD_DIM], lhsT=ones[:], rhs=gain_row[:], start=True, stop=True)
+        idle_bank = psum_q.tile([P, BANK], F32, tag="q_bank")
+
+        def keep_warm():
+            nc.tensor.matmul(out=idle_bank[:, :P], lhsT=identity[:], rhs=identity[:], start=True, stop=True)
+
+        for i in range(7):
+            keep_warm()
+
         gain = keep.tile([P, HEAD_DIM], F32)
-        nc.vector.tensor_copy(out=gain[:], in_=gain_bank[:, :HEAD_DIM])
 
         rot = keep.tile([P, TABLES, 2 * HEAD_DIM], F32)
         gain_parts = gain[:].rearrange("p (j a) -> p a j", a=2)
@@ -126,7 +129,14 @@ def tile_mla_pb_t_kernel(tc, x, wq, q_norm_w, freqs_cos, freqs_sin, out):
                     op=ALU.mult,
                 )
 
-        make_tables(0, GROUP)
+        def spread_gain():
+            ones = keep.tile([P, P], BF16)
+            nc.vector.memset(ones[:], 1.0)
+            gain_bank = psum_q.tile([P, BANK], F32, tag="q_bank")
+            nc.tensor.matmul(out=gain_bank[:, :HEAD_DIM], lhsT=ones[:], rhs=gain_row[:], start=True, stop=True)
+            nc.vector.tensor_copy(out=gain[:], in_=gain_bank[:, :HEAD_DIM])
+            make_tables(0, GROUP)
+
 
         def turn(rows, selector):
             turned = psum_turned.tile([P, WORD_BLOCKS, P], F32)
@@ -337,6 +347,8 @@ def tile_mla_pb_t_kernel(tc, x, wq, q_norm_w, freqs_cos, freqs_sin, out):
             if step >= 11:
                 transpose_item(step + 1)
                 regroup_item(step)
+            if step in range(6):
+                keep_warm()
             if step in squares:
                 square_early(squares[step])
                 invert_early(squares[step])
@@ -346,6 +358,8 @@ def tile_mla_pb_t_kernel(tc, x, wq, q_norm_w, freqs_cos, freqs_sin, out):
                     invert_bank(EARLY_TILES, b)
             if step < 11:
                 transpose_item(step + 1)
+                if step == 0:
+                    spread_gain()
                 regroup_item(step)
             if step in rotations:
                 rotate_early(rotations[step])

@@ -55,6 +55,8 @@ def tile_mla_pb_t_kernel(tc, x, wq, q_norm_w, freqs_cos, freqs_sin, out):
         psum_q = stack.enter_context(tc.psum_pool(name="psum_q", bufs=5))
         stack.enter_context(tc.manual_schedule())
 
+        ones = keep.tile([P, P], BF16)
+        nc.vector.memset(ones[:], 1.0)
         gain_row = keep.tile([P, HEAD_DIM], BF16)
         nc.vector.memset(gain_row[:], 0.0)
         trig = keep.tile([P, 3, TABLES * PAIRS], BF16)
@@ -97,6 +99,20 @@ def tile_mla_pb_t_kernel(tc, x, wq, q_norm_w, freqs_cos, freqs_sin, out):
         first_use = keep.tile([P, 1], F32)
         nc.scalar.activation(out=first_use[:], in_=eps[:], func=ACT.Abs_reciprocal_sqrt)
 
+        idle_bank = psum_q.tile([P, BANK], F32, tag="q_bank")
+
+        def keep_warm():
+            nc.tensor.matmul(
+                out=idle_bank[:].rearrange("p (i f) -> p i f", f=P),
+                lhsT=ones[:],
+                rhs=ones[:].unsqueeze(1).to_broadcast([P, BANK // P, P]),
+                start=True,
+                stop=True,
+            )
+
+        for i in range(5):
+            keep_warm()
+
         identity = keep.tile([P, P], F32)
         make_identity(nc, identity[:])
         evens_first = keep.tile([P, P], F32)
@@ -104,14 +120,6 @@ def tile_mla_pb_t_kernel(tc, x, wq, q_norm_w, freqs_cos, freqs_sin, out):
             out=evens_first[:].rearrange("p (a j) -> p a j", a=2),
             in_=identity[:].rearrange("p (j a) -> p a j", a=2),
         )
-
-        idle_bank = psum_q.tile([P, BANK], F32, tag="q_bank")
-
-        def keep_warm():
-            nc.tensor.matmul(out=idle_bank[:, :P], lhsT=identity[:], rhs=identity[:], start=True, stop=True)
-
-        for i in range(7):
-            keep_warm()
 
         gain = keep.tile([P, HEAD_DIM], F32)
 
@@ -130,8 +138,6 @@ def tile_mla_pb_t_kernel(tc, x, wq, q_norm_w, freqs_cos, freqs_sin, out):
                 )
 
         def spread_gain():
-            ones = keep.tile([P, P], BF16)
-            nc.vector.memset(ones[:], 1.0)
             gain_bank = psum_q.tile([P, BANK], F32, tag="q_bank")
             nc.tensor.matmul(out=gain_bank[:, :HEAD_DIM], lhsT=ones[:], rhs=gain_row[:], start=True, stop=True)
             nc.vector.tensor_copy(out=gain[:], in_=gain_bank[:, :HEAD_DIM])
@@ -347,7 +353,7 @@ def tile_mla_pb_t_kernel(tc, x, wq, q_norm_w, freqs_cos, freqs_sin, out):
             if step >= 11:
                 transpose_item(step + 1)
                 regroup_item(step)
-            if step in range(6):
+            if step in (2, 4):
                 keep_warm()
             if step in squares:
                 square_early(squares[step])

@@ -261,6 +261,11 @@ def tile_mla_pb_t_kernel(tc, x, wq, q_norm_w, freqs_cos, freqs_sin, out):
             heads = slice(b * HEADS_PER_BANK, (b + 1) * HEADS_PER_BANK)
             invert_rms(inverse_of["tile", n][:, heads], squares_of["tile", n][:, heads])
 
+        def invert_tile(n):
+            inverse = stage.tile([P, HEADS], F32)
+            invert_rms(inverse[:], squares_of["tile", n][:])
+            inverse_of["tile", n] = inverse
+
         def multiply_by_table(n, q, inverse, products):
             nc.vector.scalar_tensor_tensor(
                 out=products.rearrange("p a (j e) -> p a j e", e=2),
@@ -386,13 +391,13 @@ def tile_mla_pb_t_kernel(tc, x, wq, q_norm_w, freqs_cos, freqs_sin, out):
             if (step - EARLY_TILES) % GROUP == 0 and group < TILES // GROUP:
                 load_x_group(group)
             when_valid(quantise_x, step + 2, 0, TILES)
-            if step + 2 < TILES:
-                multiply_bank(step + 2, 0)
             when_valid(transpose_x, step + AHEAD, 0, TILES)
             when_valid(square_tile, step + 1, 0, TILES)
-            if step + 1 < TILES:
-                invert_bank(step + 1, 0)
             when_valid(regroup_x, step + 3, 0, TILES)
-            if step + 1 < TILES:
-                invert_bank(step + 1, 1)
-            rotate_tile(step, lambda n=step + 2: multiply_bank(n, 1) if n < TILES else None)
+            when_valid(invert_tile, step + 1, 0, TILES)
+            def multiply_next(n=step + 2):
+                if n < TILES:
+                    for b in range(BANKS):
+                        multiply_bank(n, b)
+
+            rotate_tile(step, multiply_next)

@@ -277,7 +277,8 @@ def tile_mla_pb_t_kernel(tc, x, wq, q_norm_w, freqs_cos, freqs_sin, out):
             )
 
         def store(n, columns, rotated):
-            nc.sync.dma_start(
+            queue = nc.scalar if n == TILES - 1 else nc.sync
+            queue.dma_start(
                 out=out_rows[n // GROUP * GROUP * P : (n // GROUP + 1) * GROUP * P, columns].rearrange("(p i) f -> p i f", i=GROUP)[
                     :, n % GROUP, :
                 ],
@@ -312,17 +313,25 @@ def tile_mla_pb_t_kernel(tc, x, wq, q_norm_w, freqs_cos, freqs_sin, out):
             for h in range(HEADS):
                 if h == HEADS_PER_BANK:
                     between_banks()
+                    if n == TILES - 2:
+                        add_and_store(nc.gpsimd, 0, 1)
                 multiply_by_table(
                     n,
                     q_of[n, h // UNIT_HEADS][:, head_columns(h % UNIT_HEADS)],
                     inverse_of["tile", n][:, h : h + 1],
                     products[:, h // HEADS_PER_BANK, :, head_columns(h % HEADS_PER_BANK)],
                 )
-            if n < TILES - 1:
+            if n < TILES - 2:
                 add_and_store(nc.gpsimd, 0, BANKS)
+            elif n == TILES - 2:
+                add_and_store(nc.gpsimd, 1, 1)
             else:
-                for b in range(BANKS):
-                    add_and_store(nc.vector, b, 1)
+                for unit in range(UNITS):
+                    half = slice(unit % (BANK // UNIT) * UNIT, (unit % (BANK // UNIT) + 1) * UNIT)
+                    parts = products[:, unit * UNIT // BANK, :, half]
+                    rotated = results.tile([P, UNIT], F32, tag="last_rotated")
+                    nc.vector.tensor_tensor(out=rotated[:], in0=parts[:, 0, :], in1=parts[:, 1, :], op=ALU.add)
+                    store(n, slice(unit * UNIT, (unit + 1) * UNIT), rotated[:])
 
         def when_valid(stage_of_item, item, first, end):
             if first <= item < end:

@@ -36,6 +36,7 @@ FLOPS = 2 * TOKENS * K * FEATURES
 UNIT_HEADS = 2
 UNITS = HEADS // UNIT_HEADS
 UNIT = UNIT_HEADS * HEAD_DIM
+ADDED_BY_TENSOR = 128
 EARLY_TILES = 2
 AHEAD = 4
 LOADED_AHEAD = 3
@@ -145,7 +146,8 @@ def tile_mla_pb_t_kernel(tc, x, wq, q_norm_w, freqs_cos, freqs_sin, out):
 
 
         def turn(rows, selector):
-            turned = psum_turned.tile([P, WORD_BLOCKS, P], F32)
+            turned_bank = psum_turned.tile([P, BANK], F32, tag="turned")
+            turned = turned_bank[:].rearrange("p (w r) -> p w r", r=P)
             words = rows.bitcast(F32)
             for g in range(PASSES):
                 first, last = g * HALVES * P, (g + 1) * HALVES * P
@@ -154,7 +156,7 @@ def tile_mla_pb_t_kernel(tc, x, wq, q_norm_w, freqs_cos, freqs_sin, out):
             return turned
 
         def regroup(copy, grouped, turned):
-            copy(out=grouped, in_=turned[:].rearrange("p (g u) r -> p g r u", u=HALVES))
+            copy(out=grouped, in_=turned.rearrange("p (g u) r -> p g r u", u=HALVES))
 
         w_codes = keep.tile([P, UNITS, PASSES, UNIT], U32, align_bytes=64)
         w_scales = keep.tile([P, UNITS, PASSES, UNIT], U8, align_bytes=64)
@@ -301,37 +303,57 @@ def tile_mla_pb_t_kernel(tc, x, wq, q_norm_w, freqs_cos, freqs_sin, out):
             for n in range(EARLY_TILES):
                 store(n, slice(unit * UNIT, (unit + 1) * UNIT), rotated[:, n, :])
 
-        def rotate_tile(n, between_banks):
-            products = work.tile([P, BANKS, 2, BANK], F32)
+        parts_of = {}
 
-            def add_and_store(adder, first_bank, banks):
-                some = slice(first_bank, first_bank + banks)
-                rotated = results.tile([P, banks, BANK], F32)
-                adder.tensor_tensor(out=rotated[:], in0=products[:, some, 0, :], in1=products[:, some, 1, :], op=ALU.add)
-                store(n, slice(first_bank * BANK, (first_bank + banks) * BANK), rotated[:].rearrange("p b f -> p (b f)"))
+        def rotate_tile(n, between_banks):
+            products = work.tile([P, 2, FEATURES], F32)
+
+            def add(adder, first, last, rotated):
+                columns = slice(first, last)
+                adder.tensor_tensor(out=rotated, in0=products[:, 0, columns], in1=products[:, 1, columns], op=ALU.add)
+
+            def add_and_store(adder, first, last):
+                rotated = results.tile([P, last - first], F32, tag="rotated_unit")
+                add(adder, first, last, rotated[:])
+                store(n, slice(first, last), rotated[:])
 
             for h in range(HEADS):
                 if h == HEADS_PER_BANK:
                     between_banks()
-                    if n == TILES - 2:
-                        add_and_store(nc.gpsimd, 0, 1)
                 multiply_by_table(
                     n,
                     q_of[n, h // UNIT_HEADS][:, head_columns(h % UNIT_HEADS)],
                     inverse_of["tile", n][:, h : h + 1],
-                    products[:, h // HEADS_PER_BANK, :, head_columns(h % HEADS_PER_BANK)],
+                    products[:, :, head_columns(h)],
                 )
-            if n < TILES - 2:
-                add_and_store(nc.gpsimd, 0, BANKS)
-            elif n == TILES - 2:
-                add_and_store(nc.gpsimd, 1, 1)
+            if n < TILES - 1:
+                rotated = results.tile([P, FEATURES], F32)
+                add(nc.gpsimd, 0, FEATURES - ADDED_BY_TENSOR, rotated[:, : FEATURES - ADDED_BY_TENSOR])
+                parts_of[n] = (products, rotated)
             else:
                 for unit in range(UNITS):
-                    half = slice(unit % (BANK // UNIT) * UNIT, (unit % (BANK // UNIT) + 1) * UNIT)
-                    parts = products[:, unit * UNIT // BANK, :, half]
-                    rotated = results.tile([P, UNIT], F32, tag="last_rotated")
-                    nc.vector.tensor_tensor(out=rotated[:], in0=parts[:, 0, :], in1=parts[:, 1, :], op=ALU.add)
-                    store(n, slice(unit * UNIT, (unit + 1) * UNIT), rotated[:])
+                    add_and_store(nc.vector, unit * UNIT, (unit + 1) * UNIT)
+
+        def add_on_tensor(n):
+            if n in parts_of:
+                sum_bank = psum_turned.tile([P, BANK], F32, tag="turned")
+                for a in range(2):
+                    nc.tensor.matmul(
+                        out=sum_bank[:, :ADDED_BY_TENSOR],
+                        lhsT=identity[:],
+                        rhs=parts_of[n][0][:, a, FEATURES - ADDED_BY_TENSOR :],
+                        start=(a == 0),
+                        stop=(a == 1),
+                    )
+                sums_of[n] = sum_bank
+
+        def store_tile(n):
+            if n in parts_of:
+                rotated = parts_of[n][1]
+                nc.scalar.copy(out=rotated[:, FEATURES - ADDED_BY_TENSOR :], in_=sums_of[n][:, :ADDED_BY_TENSOR])
+                store(n, slice(0, FEATURES), rotated[:])
+
+        sums_of = {}
 
         def when_valid(stage_of_item, item, first, end):
             if first <= item < end:
@@ -401,9 +423,11 @@ def tile_mla_pb_t_kernel(tc, x, wq, q_norm_w, freqs_cos, freqs_sin, out):
                 load_x_group(group)
             when_valid(quantise_x, step + 2, 0, TILES)
             when_valid(transpose_x, step + AHEAD, 0, TILES)
-            when_valid(square_tile, step + 1, 0, TILES)
             when_valid(regroup_x, step + 3, 0, TILES)
+            add_on_tensor(step - 1)
+            when_valid(square_tile, step + 1, 0, TILES)
             when_valid(invert_tile, step + 1, 0, TILES)
+            store_tile(step - 1)
             def multiply_next(n=step + 2):
                 if n < TILES:
                     for b in range(BANKS):

@@ -111,7 +111,7 @@ def tile_mla_pb_t_kernel(tc, x, wq, q_norm_w, freqs_cos, freqs_sin, out):
                 stop=True,
             )
 
-        for i in range(5):
+        for i in range(6):
             keep_warm()
 
         identity = keep.tile([P, P], F32)
@@ -389,7 +389,7 @@ def tile_mla_pb_t_kernel(tc, x, wq, q_norm_w, freqs_cos, freqs_sin, out):
             if step >= 11:
                 transpose_item(step + 1)
                 regroup_item(step)
-            if step in (2, 4):
+            if step in range(1, 5):
                 keep_warm()
             if step in squares:
                 square_early(squares[step])

@@ -305,53 +305,63 @@ def tile_mla_pb_t_kernel(tc, x, wq, q_norm_w, freqs_cos, freqs_sin, out):
 
         parts_of = {}
 
+        def add_on_vector_or_gpsimd(adder, products, columns, rotated):
+            adder.tensor_tensor(out=rotated, in0=products[:, 0, columns], in1=products[:, 1, columns], op=ALU.add)
+
+        def add_on_tensor(products, columns):
+            sum_bank = psum_turned.tile([P, BANK], F32, tag="turned")
+            width = columns.stop - columns.start
+            for a in range(2):
+                nc.tensor.matmul(
+                    out=sum_bank[:, :width], lhsT=identity[:], rhs=products[:, a, columns], start=(a == 0), stop=(a == 1)
+                )
+            return sum_bank[:, :width]
+
+        def multiply_head(n, h, products):
+            multiply_by_table(
+                n, q_of[n, h // UNIT_HEADS][:, head_columns(h % UNIT_HEADS)], inverse_of["tile", n][:, h : h + 1], products
+            )
+
         def rotate_tile(n, between_banks):
             products = work.tile([P, 2, FEATURES], F32)
-
-            def add(adder, first, last, rotated):
-                columns = slice(first, last)
-                adder.tensor_tensor(out=rotated, in0=products[:, 0, columns], in1=products[:, 1, columns], op=ALU.add)
-
-            def add_and_store(adder, first, last):
-                rotated = results.tile([P, last - first], F32, tag="rotated_unit")
-                add(adder, first, last, rotated[:])
-                store(n, slice(first, last), rotated[:])
-
             for h in range(HEADS):
                 if h == HEADS_PER_BANK:
                     between_banks()
-                multiply_by_table(
-                    n,
-                    q_of[n, h // UNIT_HEADS][:, head_columns(h % UNIT_HEADS)],
-                    inverse_of["tile", n][:, h : h + 1],
-                    products[:, :, head_columns(h)],
-                )
-            if n < TILES - 1:
-                rotated = results.tile([P, FEATURES], F32)
-                add(nc.gpsimd, 0, FEATURES - ADDED_BY_TENSOR, rotated[:, : FEATURES - ADDED_BY_TENSOR])
-                parts_of[n] = (products, rotated)
-            else:
-                for unit in range(UNITS):
-                    add_and_store(nc.vector, unit * UNIT, (unit + 1) * UNIT)
+                multiply_head(n, h, products[:, :, head_columns(h)])
+            rotated = results.tile([P, FEATURES], F32)
+            columns = slice(0, FEATURES - ADDED_BY_TENSOR)
+            add_on_vector_or_gpsimd(nc.gpsimd, products, columns, rotated[:, columns])
+            parts_of[n] = (products, rotated)
 
-        def add_on_tensor(n):
-            if n in parts_of:
-                sum_bank = psum_turned.tile([P, BANK], F32, tag="turned")
-                for a in range(2):
-                    nc.tensor.matmul(
-                        out=sum_bank[:, :ADDED_BY_TENSOR],
-                        lhsT=identity[:],
-                        rhs=parts_of[n][0][:, a, FEATURES - ADDED_BY_TENSOR :],
-                        start=(a == 0),
-                        stop=(a == 1),
-                    )
-                sums_of[n] = sum_bank
+        def add_rest(n):
+            if EARLY_TILES <= n < TILES - 2:
+                sums_of[n] = add_on_tensor(parts_of[n][0], slice(FEATURES - ADDED_BY_TENSOR, FEATURES))
 
         def store_tile(n):
-            if n in parts_of:
+            if EARLY_TILES <= n < TILES - 2:
                 rotated = parts_of[n][1]
-                nc.scalar.copy(out=rotated[:, FEATURES - ADDED_BY_TENSOR :], in_=sums_of[n][:, :ADDED_BY_TENSOR])
+                nc.scalar.copy(out=rotated[:, FEATURES - ADDED_BY_TENSOR :], in_=sums_of[n])
                 store(n, slice(0, FEATURES), rotated[:])
+
+        def rotate_by_units(n, adders):
+            products = results.tile([P, UNITS, 2, UNIT], F32, tag="last_products")
+            rotated = results.tile([P, UNITS, UNIT], F32, tag="last_rotated")
+
+            def add_and_store(unit):
+                if adders[unit] == nc.tensor:
+                    nc.scalar.copy(out=rotated[:, unit, :], in_=add_on_tensor(products[:, unit, :, :], slice(0, UNIT)))
+                else:
+                    add_on_vector_or_gpsimd(adders[unit], products[:, unit, :, :], slice(0, UNIT), rotated[:, unit, :])
+                store(n, slice(unit * UNIT, (unit + 1) * UNIT), rotated[:, unit, :])
+
+            for unit in range(UNITS):
+                for i in range(UNIT_HEADS):
+                    multiply_head(n, unit * UNIT_HEADS + i, products[:, unit, :, head_columns(i)])
+                if adders[unit] != nc.vector:
+                    add_and_store(unit)
+            for unit in range(UNITS):
+                if adders[unit] == nc.vector:
+                    add_and_store(unit)
 
         sums_of = {}
 
@@ -424,7 +434,7 @@ def tile_mla_pb_t_kernel(tc, x, wq, q_norm_w, freqs_cos, freqs_sin, out):
             when_valid(quantise_x, step + 2, 0, TILES)
             when_valid(transpose_x, step + AHEAD, 0, TILES)
             when_valid(regroup_x, step + 3, 0, TILES)
-            add_on_tensor(step - 1)
+            add_rest(step - 1)
             when_valid(square_tile, step + 1, 0, TILES)
             when_valid(invert_tile, step + 1, 0, TILES)
             store_tile(step - 1)
@@ -433,4 +443,9 @@ def tile_mla_pb_t_kernel(tc, x, wq, q_norm_w, freqs_cos, freqs_sin, out):
                     for b in range(BANKS):
                         multiply_bank(n, b)
 
-            rotate_tile(step, multiply_next)
+            if step < TILES - 2:
+                rotate_tile(step, multiply_next)
+            elif step == TILES - 2:
+                rotate_by_units(step, (nc.gpsimd, nc.gpsimd, nc.gpsimd, nc.tensor))
+            else:
+                rotate_by_units(step, (nc.tensor, nc.gpsimd, nc.vector, nc.vector))

from contextlib import ExitStack

import concourse.mybir as mybir
from concourse.masks import make_identity

F32 = mybir.dt.float32
BF16 = mybir.dt.bfloat16
U32 = mybir.dt.uint32
U8 = mybir.dt.uint8
FP8X4 = mybir.dt.float8_e4m3fn_x4
ACT = mybir.ActivationFunctionType
ALU = mybir.AluOpType

P = 128
TOKENS = 4 * 1024
SEQUENCE = 1024
K = 1024
HEADS = 8
HEAD_DIM = 128
PAIRS = HEAD_DIM // 2
FEATURES = HEADS * HEAD_DIM
EPS = 1e-6

PACK = 4
PASSES = K // (P * PACK)
HALVES = 2
WORD_BLOCKS = PASSES * HALVES
BANK = 512
BANKS = FEATURES // BANK
HEADS_PER_BANK = BANK // HEAD_DIM
GROUP = 4
TILES = TOKENS // P
TABLES = SEQUENCE // P

FLOPS = 2 * TOKENS * K * FEATURES
UNIT_HEADS = 2
UNITS = HEADS // UNIT_HEADS
UNIT = UNIT_HEADS * HEAD_DIM
ADDED_BY_TENSOR = 128
EARLY_TILES = 2
AHEAD = 4
LOADED_AHEAD = 3


def tile_mla_pb_t_kernel(tc, x, wq, q_norm_w, freqs_cos, freqs_sin, out):
    nc = tc.nc
    x_rows = x.flatten_outer_dims()
    out_rows = out.rearrange("b t h d -> (b t) (h d)")

    with ExitStack() as stack:
        keep = stack.enter_context(tc.tile_pool(name="keep", bufs=1))
        stage = stack.enter_context(tc.tile_pool(name="stage", bufs=3))
        work = stack.enter_context(tc.tile_pool(name="work", bufs=3))
        results = stack.enter_context(tc.tile_pool(name="results", bufs=4))
        psum_turned = stack.enter_context(tc.psum_pool(name="psum_turned", bufs=3))
        psum_q = stack.enter_context(tc.psum_pool(name="psum_q", bufs=5))
        stack.enter_context(tc.manual_schedule())

        ones = keep.tile([P, P], BF16)
        nc.vector.memset(ones[:], 1.0)
        gain_row = keep.tile([P, HEAD_DIM], BF16)
        nc.vector.memset(gain_row[:], 0.0)
        trig = keep.tile([P, 3, TABLES * PAIRS], BF16)

        def load_trig(queue, s):
            columns = slice(s * GROUP * PAIRS, (s + 1) * GROUP * PAIRS)
            for k, freqs in ((1, freqs_cos), (2, freqs_sin)):
                queue.dma_start(out=trig[:, k, columns], in_=freqs[s * GROUP * P : (s + 1) * GROUP * P, :].rearrange("(p i) j -> p (i j)", i=GROUP))

        load_trig(nc.scalar, 0)
        wq_sb = keep.tile([P, HEADS, K], BF16)
        wq_by_head = wq.rearrange("(h p) k -> p h k", p=P)
        x_sb = keep.tile([P, TILES, K], BF16)

        def group_rows(group):
            first = group * GROUP
            return x_rows[first * P : (first + GROUP) * P, :].rearrange("(p i) k -> p i k", i=GROUP)

        def load_x_tile(n):
            nc.sync.dma_start(out=x_sb[:, n, :], in_=group_rows(n // GROUP)[:, n % GROUP, :])

        def load_x_group(group):
            nc.sync.dma_start(out=x_sb[:, group * GROUP : (group + 1) * GROUP, :], in_=group_rows(group))

        for h in range(HEADS):
            nc.sync.dma_start(out=wq_sb[:, h, :], in_=wq_by_head[:, h, :])
            if h == 0:
                nc.sync.dma_start(out=gain_row[0:1, :], in_=q_norm_w.unsqueeze(0))
            if h < EARLY_TILES:
                load_x_tile(h)
            if h == 3:
                load_trig(nc.sync, 1)
        for n in range(EARLY_TILES, GROUP):
            load_x_tile(n)
        for group in range(1, LOADED_AHEAD):
            load_x_group(group)

        eps = keep.tile([P, 1], F32)
        nc.vector.memset(eps[:], EPS)
        first_use = keep.tile([P, 1], F32)
        nc.scalar.activation(out=first_use[:], in_=eps[:], func=ACT.Abs_reciprocal_sqrt)

        idle_bank = psum_q.tile([P, BANK], F32, tag="q_bank")

        def keep_warm():
            nc.tensor.matmul(
                out=idle_bank[:].rearrange("p (i f) -> p i f", f=P),
                lhsT=ones[:],
                rhs=ones[:].unsqueeze(1).to_broadcast([P, BANK // P, P]),
                start=True,
                stop=True,
            )

        for i in range(6):
            keep_warm()

        identity = keep.tile([P, P], F32)
        make_identity(nc, identity[:])
        evens_first = keep.tile([P, P], F32)
        nc.vector.tensor_copy(
            out=evens_first[:].rearrange("p (a j) -> p a j", a=2),
            in_=identity[:].rearrange("p (j a) -> p a j", a=2),
        )

        gain = keep.tile([P, HEAD_DIM], F32)

        rot = keep.tile([P, TABLES, 2 * HEAD_DIM], F32)
        gain_parts = gain[:].rearrange("p (j a) -> p a j", a=2)

        def make_tables(first, last):
            columns = slice(first * PAIRS, last * PAIRS)
            nc.vector.tensor_scalar(out=trig[:, 0, columns], in0=trig[:, 2, columns], scalar1=-1.0, scalar2=None, op0=ALU.mult)
            for a in range(2):
                nc.vector.tensor_tensor(
                    out=rot[:, first:last, a * HEAD_DIM : (a + 1) * HEAD_DIM].rearrange("p m (j e) -> p m j e", e=2),
                    in0=trig[:, 1 - a : 3 - a, first * PAIRS : last * PAIRS].rearrange("p e (m j) -> p m j e", j=PAIRS),
                    in1=gain_parts[:, a].unsqueeze(1).unsqueeze(3).to_broadcast([P, last - first, PAIRS, 2]),
                    op=ALU.mult,
                )

        def spread_gain():
            gain_bank = psum_q.tile([P, BANK], F32, tag="q_bank")
            nc.tensor.matmul(out=gain_bank[:, :HEAD_DIM], lhsT=ones[:], rhs=gain_row[:], start=True, stop=True)
            nc.vector.tensor_copy(out=gain[:], in_=gain_bank[:, :HEAD_DIM])
            make_tables(0, GROUP)


        def turn(rows, selector):
            turned_bank = psum_turned.tile([P, BANK], F32, tag="turned")
            turned = turned_bank[:].rearrange("p (w r) -> p w r", r=P)
            words = rows.bitcast(F32)
            for g in range(PASSES):
                first, last = g * HALVES * P, (g + 1) * HALVES * P
                for u in range(HALVES):
                    nc.tensor.transpose(turned[:, g * HALVES + u, :], words[:, first + u : last : HALVES], selector[:])
            return turned

        def regroup(copy, grouped, turned):
            copy(out=grouped, in_=turned.rearrange("p (g u) r -> p g r u", u=HALVES))

        w_codes = keep.tile([P, UNITS, PASSES, UNIT], U32, align_bytes=64)
        w_scales = keep.tile([P, UNITS, PASSES, UNIT], U8, align_bytes=64)
        w_turned_of, w_grouped_of = {}, {}

        def transpose_w(h):
            w_turned_of[h] = turn(wq_sb[:, h, :], evens_first)

        def regroup_w(h):
            if h % UNIT_HEADS == 0:
                w_grouped = work.tile([P, PASSES * UNIT * PACK], BF16, align_bytes=64)
                w_grouped_of[h // UNIT_HEADS] = w_grouped
            words = w_grouped_of[h // UNIT_HEADS][:].bitcast(F32)
            by_head = words.rearrange("p (g i r u) -> p g i r u", g=PASSES, i=UNIT_HEADS, u=HALVES)
            regroup(nc.scalar.copy, by_head[:, :, h % UNIT_HEADS], w_turned_of[h])

        def quantise_w(unit):
            nc.vector.quantize_mx(
                out=w_codes[:, unit, :, :].rearrange("p g f -> p (g f)").bitcast(FP8X4),
                scales=w_scales[:, unit, :, :].rearrange("p g f -> p (g f)"),
                in_=w_grouped_of[unit][:],
            )

        turned_of, grouped_of, codes_of, scales_of = {}, {}, {}, {}

        def transpose_x(n):
            turned_of[n] = turn(x_sb[:, n, :], identity)

        def regroup_x(n):
            x_grouped = stage.tile([P, PASSES * P * PACK], BF16, align_bytes=64)
            words = x_grouped[:].bitcast(F32).rearrange("p (g r u) -> p g r u", g=PASSES, u=HALVES)
            regroup(nc.scalar.copy, words, turned_of[n])
            grouped_of[n] = x_grouped

        def quantise_x(n):
            x_codes = stage.tile([P, PASSES * P], U32, align_bytes=64)
            x_scales = stage.tile([P, PASSES * P], U8, align_bytes=64)
            nc.vector.quantize_mx(out=x_codes[:].bitcast(FP8X4), scales=x_scales[:], in_=grouped_of[n][:])
            codes_of[n], scales_of[n] = x_codes, x_scales

        q_of, squares_of, inverse_of = {}, {}, {}

        def multiply(n, unit, q):
            for g in range(PASSES):
                tokens = slice(g * P, (g + 1) * P)
                nc.tensor.matmul_mx(
                    out=q,
                    lhsT=codes_of[n][:, tokens].bitcast(FP8X4),
                    lhsT_scale=scales_of[n][:, tokens],
                    rhs=w_codes[:, unit, g, :].bitcast(FP8X4),
                    rhs_scale=w_scales[:, unit, g, :],
                    start=(g == 0),
                    stop=(g == PASSES - 1),
                )
            q_of[n, unit] = q

        def multiply_early(unit):
            for n in range(EARLY_TILES):
                q_bank = psum_q.tile([P, BANK], F32, tag="q_bank")
                multiply(n, unit, q_bank[:, :UNIT])

        def multiply_bank(n, b):
            q_bank = psum_q.tile([P, BANK], F32, tag="q_bank")
            for part in range(BANK // UNIT):
                multiply(n, b * BANK // UNIT + part, q_bank[:, part * UNIT : (part + 1) * UNIT])

        def head_columns(i):
            return slice(i * HEAD_DIM, (i + 1) * HEAD_DIM)

        def square_unit(n, unit, sums):
            unread = stage.tile([P, UNIT], BF16)
            for i in range(UNIT_HEADS):
                nc.scalar.activation(
                    out=unread[:, head_columns(i)],
                    in_=q_of[n, unit][:, head_columns(i)],
                    func=ACT.Square,
                    accum_out=sums[:, i : i + 1],
                )

        def invert_rms(inverse, squares):
            nc.scalar.activation(out=inverse, in_=squares, func=ACT.Abs_reciprocal_sqrt, scale=1.0 / HEAD_DIM, bias=eps[:])

        def square_early(unit):
            squares = stage.tile([P, EARLY_TILES * UNIT_HEADS], F32, tag="early_squares")
            for n in range(EARLY_TILES):
                square_unit(n, unit, squares[:, n * UNIT_HEADS : (n + 1) * UNIT_HEADS])
            squares_of[unit] = squares

        def invert_early(unit):
            inverse = stage.tile([P, EARLY_TILES * UNIT_HEADS], F32, tag="early_inverse")
            invert_rms(inverse[:], squares_of[unit][:])
            inverse_of[unit] = inverse

        def square_tile(n):
            squares = stage.tile([P, HEADS], F32)
            for unit in range(UNITS):
                square_unit(n, unit, squares[:, unit * UNIT_HEADS : (unit + 1) * UNIT_HEADS])
            squares_of["tile", n] = squares

        def invert_bank(n, b):
            if b == 0:
                inverse = stage.tile([P, HEADS], F32)
                inverse_of["tile", n] = inverse
            heads = slice(b * HEADS_PER_BANK, (b + 1) * HEADS_PER_BANK)
            invert_rms(inverse_of["tile", n][:, heads], squares_of["tile", n][:, heads])

        def invert_tile(n):
            inverse = stage.tile([P, HEADS], F32)
            invert_rms(inverse[:], squares_of["tile", n][:])
            inverse_of["tile", n] = inverse

        def multiply_by_table(n, q, inverse, products):
            nc.vector.scalar_tensor_tensor(
                out=products.rearrange("p a (j e) -> p a j e", e=2),
                in0=q.rearrange("p (a j) -> p a j", a=2).unsqueeze(3).to_broadcast([P, 2, PAIRS, 2]),
                scalar=inverse,
                in1=rot[:, n % TABLES, :].rearrange("p (a j e) -> p a j e", a=2, e=2),
                op0=ALU.mult,
                op1=ALU.mult,
            )

        def store(n, columns, rotated):
            queue = nc.scalar if n == TILES - 1 else nc.sync
            queue.dma_start(
                out=out_rows[n // GROUP * GROUP * P : (n // GROUP + 1) * GROUP * P, columns].rearrange("(p i) f -> p i f", i=GROUP)[
                    :, n % GROUP, :
                ],
                in_=rotated,
            )

        def rotate_early(unit):
            products = work.tile([P, EARLY_TILES, 2, UNIT], F32, tag="early_products")
            for n in range(EARLY_TILES):
                for i in range(UNIT_HEADS):
                    column = n * UNIT_HEADS + i
                    multiply_by_table(
                        n,
                        q_of[n, unit][:, head_columns(i)],
                        inverse_of[unit][:, column : column + 1],
                        products[:, n, :, head_columns(i)],
                    )
            rotated = results.tile([P, EARLY_TILES, UNIT], F32, tag="early_rotated")
            nc.gpsimd.tensor_tensor(out=rotated[:], in0=products[:, :, 0, :], in1=products[:, :, 1, :], op=ALU.add)
            for n in range(EARLY_TILES):
                store(n, slice(unit * UNIT, (unit + 1) * UNIT), rotated[:, n, :])

        parts_of = {}

        def add_on_vector_or_gpsimd(adder, products, columns, rotated):
            adder.tensor_tensor(out=rotated, in0=products[:, 0, columns], in1=products[:, 1, columns], op=ALU.add)

        def add_on_tensor(products, columns):
            sum_bank = psum_turned.tile([P, BANK], F32, tag="turned")
            width = columns.stop - columns.start
            for a in range(2):
                nc.tensor.matmul(
                    out=sum_bank[:, :width], lhsT=identity[:], rhs=products[:, a, columns], start=(a == 0), stop=(a == 1)
                )
            return sum_bank[:, :width]

        def multiply_head(n, h, products):
            multiply_by_table(
                n, q_of[n, h // UNIT_HEADS][:, head_columns(h % UNIT_HEADS)], inverse_of["tile", n][:, h : h + 1], products
            )

        def rotate_tile(n, between_banks):
            products = work.tile([P, 2, FEATURES], F32)
            for h in range(HEADS):
                if h == HEADS_PER_BANK:
                    between_banks()
                multiply_head(n, h, products[:, :, head_columns(h)])
            rotated = results.tile([P, FEATURES], F32)
            columns = slice(0, FEATURES - ADDED_BY_TENSOR)
            add_on_vector_or_gpsimd(nc.gpsimd, products, columns, rotated[:, columns])
            parts_of[n] = (products, rotated)

        def add_rest(n):
            if EARLY_TILES <= n < TILES - 2:
                sums_of[n] = add_on_tensor(parts_of[n][0], slice(FEATURES - ADDED_BY_TENSOR, FEATURES))

        def store_tile(n):
            if EARLY_TILES <= n < TILES - 2:
                rotated = parts_of[n][1]
                nc.scalar.copy(out=rotated[:, FEATURES - ADDED_BY_TENSOR :], in_=sums_of[n])
                store(n, slice(0, FEATURES), rotated[:])

        def rotate_by_units(n, adders):
            products = results.tile([P, UNITS, 2, UNIT], F32, tag="last_products")
            rotated = results.tile([P, UNITS, UNIT], F32, tag="last_rotated")

            def add_and_store(unit):
                if adders[unit] == nc.tensor:
                    nc.scalar.copy(out=rotated[:, unit, :], in_=add_on_tensor(products[:, unit, :, :], slice(0, UNIT)))
                else:
                    add_on_vector_or_gpsimd(adders[unit], products[:, unit, :, :], slice(0, UNIT), rotated[:, unit, :])
                store(n, slice(unit * UNIT, (unit + 1) * UNIT), rotated[:, unit, :])

            for unit in range(UNITS):
                for i in range(UNIT_HEADS):
                    multiply_head(n, unit * UNIT_HEADS + i, products[:, unit, :, head_columns(i)])
                if adders[unit] != nc.vector:
                    add_and_store(unit)
            for unit in range(UNITS):
                if adders[unit] == nc.vector:
                    add_and_store(unit)

        sums_of = {}

        def when_valid(stage_of_item, item, first, end):
            if first <= item < end:
                stage_of_item(item)

        items = []
        for h in range(HEADS):
            items.append((transpose_w, regroup_w, h))
            if h < EARLY_TILES:
                items.append((transpose_x, regroup_x, h))
        for n in range(EARLY_TILES, TILES):
            items.append((transpose_x, regroup_x, n))

        def transpose_item(i):
            items[i][0](items[i][2])

        def regroup_item(i):
            items[i][1](items[i][2])

        rotations = {8: 0, 10: 1, 11: 2, 12: 3}
        squares = {6: 0, 8: 1, 10: 2, 11: 3}
        transpose_item(0)
        for step in range(13):
            if step % 2 == 0 and 4 <= step <= 10:
                quantise_w((step - 4) // 2)
            if step == 4:
                for n in range(EARLY_TILES):
                    quantise_x(n)
            if step >= 11:
                quantise_x(step - 9)
            if step in (5, 7):
                multiply_early((step - 5) // 2)
            if step >= 11:
                transpose_item(step + 1)
                regroup_item(step)
            if step in range(1, 5):
                keep_warm()
            if step in squares:
                square_early(squares[step])
                invert_early(squares[step])
            if step == 12:
                square_tile(EARLY_TILES)
                for b in range(BANKS):
                    invert_bank(EARLY_TILES, b)
            if step < 11:
                transpose_item(step + 1)
                if step == 0:
                    spread_gain()
                regroup_item(step)
            if step in rotations:
                rotate_early(rotations[step])
                if rotations[step] < 2:
                    multiply_early(rotations[step] + 2)
            if step == 11:
                multiply_bank(EARLY_TILES, 0)
                multiply_bank(EARLY_TILES, 1)
            if step == 12:
                multiply_bank(EARLY_TILES + 1, 0)
                multiply_bank(EARLY_TILES + 1, 1)
            if step == 7:
                make_tables(GROUP, TABLES)


        for step in range(EARLY_TILES, TILES):
            group = LOADED_AHEAD + (step - EARLY_TILES) // GROUP
            if (step - EARLY_TILES) % GROUP == 0 and group < TILES // GROUP:
                load_x_group(group)
            when_valid(quantise_x, step + 2, 0, TILES)
            when_valid(transpose_x, step + AHEAD, 0, TILES)
            when_valid(regroup_x, step + 3, 0, TILES)
            add_rest(step - 1)
            when_valid(square_tile, step + 1, 0, TILES)
            when_valid(invert_tile, step + 1, 0, TILES)
            store_tile(step - 1)
            def multiply_next(n=step + 2):
                if n < TILES:
                    for b in range(BANKS):
                        multiply_bank(n, b)

            if step < TILES - 2:
                rotate_tile(step, multiply_next)
            elif step == TILES - 2:
                rotate_by_units(step, (nc.gpsimd, nc.gpsimd, nc.gpsimd, nc.tensor))
            else:
                rotate_by_units(step, (nc.tensor, nc.gpsimd, nc.vector, nc.vector))
